import numpy as np
import ml_dtypes


def mxq(x, axis, fmt="e4m3"):
    dtype, down = {"e4m3": (ml_dtypes.float8_e4m3fn, 7), "e5m2": (ml_dtypes.float8_e5m2, 14)}[fmt]
    v = np.moveaxis(np.asarray(x, np.float32).astype(ml_dtypes.bfloat16).astype(np.float64), axis, -1)
    blocks = v.reshape(v.shape[:-1] + (-1, 32))
    amax = np.abs(blocks).max(-1, keepdims=True)
    byte = np.maximum(np.where(amax > 0, np.frexp(amax)[1] - 1 + 127, 0) - down, 1)
    scale = np.exp2(byte - 127.0)
    codes = (blocks / scale).astype(np.float32).astype(dtype).astype(np.float64)
    return np.moveaxis((codes * scale).reshape(v.shape), -1, axis)


WIDE = False


def mx_kscale(k):
    if not WIDE:
        return np.ones(k)
    levels = np.array([10, -10, 5, -5, 0])
    a = np.random.permutation(np.resize(levels, k // 512 * 4)).reshape(k // 512, 4)
    idx = np.arange(k)
    return np.exp2(a[idx // 512, idx % 128 // 32])


BF16 = ml_dtypes.bfloat16


def bf(x):
    return np.asarray(x, np.float32).astype(BF16)


def f64(x):
    return np.asarray(x).astype(np.float64)


B, S, HIDDEN, NUM_HEADS, HEAD_DIM = 2, 512, 1024, 16, 64
F = NUM_HEADS * HEAD_DIM


def _split_heads(x):
    b, s, _ = x.shape
    return x.reshape(b, s, NUM_HEADS, HEAD_DIM).transpose(0, 2, 1, 3)


def setup_inputs():
    s = mx_kscale(HIDDEN)
    scale = 1.0 / np.sqrt(HIDDEN)
    return {
        "hidden_states": bf(np.random.standard_normal((B, S, HIDDEN)) * s),
        "Wq": bf(np.random.standard_normal((HIDDEN, F)) * scale / s[:, None]),
        "bq": bf(np.random.standard_normal(F) * 0.5),
        "Wk": bf(np.random.standard_normal((HIDDEN, F)) * scale / s[:, None]),
        "bk": bf(np.random.standard_normal(F) * 0.5),
        "Wv": bf(np.random.standard_normal((HIDDEN, F)) * scale / s[:, None]),
        "bv": bf(np.random.standard_normal(F) * 0.5),
    }


def reference(hidden_states, Wq, bq, Wk, bk, Wv, bv):
    Wqkv = np.concatenate([f64(Wq), f64(Wk), f64(Wv)], axis=1)
    bqkv = np.concatenate([f64(bq), f64(bk), f64(bv)], axis=0)
    qkv = (mxq(f64(hidden_states), 2, "e4m3") @ mxq(Wqkv, 0, "e4m3")) + bqkv
    q, k, v = np.split(qkv, 3, axis=-1)
    return (_split_heads(q), _split_heads(k), _split_heads(v))

@@ -1,0 +1,243 @@
+from contextlib import ExitStack
+
+import concourse.mybir as mybir
+from concourse.masks import make_identity
+
+F32 = mybir.dt.float32
+BF16 = mybir.dt.bfloat16
+U32 = mybir.dt.uint32
+U8 = mybir.dt.uint8
+I32 = mybir.dt.int32
+FP8X4 = mybir.dt.float8_e4m3fn_x4
+ADD = mybir.AluOpType.add
+
+P = 128
+BATCH = 2
+SEQ = 512
+HIDDEN = 1024
+HEADS = 16
+HEAD_DIM = 64
+FEATURES = HEADS * HEAD_DIM
+PASSES = HIDDEN // 512
+TOK = 8
+N_BLK = 512
+BLK_HEADS = N_BLK // HEAD_DIM
+BLOCKS = 3 * FEATURES // N_BLK
+Q_POS = 4
+
+FLOPS = 2 * BATCH * SEQ * HIDDEN * 3 * FEATURES
+
+
+def tile_attention_before_kernel(
+    tc, hidden_states, Wq, bq, Wk, bk, Wv, bv, out_0, out_1, out_2
+):
+    nc = tc.nc
+    weights = (Wq, Wk, Wv)
+    biases = (bq, bk, bv)
+    outs = (out_0, out_1, out_2)
+
+    with ExitStack() as ctx:
+        keep = ctx.enter_context(tc.tile_pool(name="keep", bufs=1))
+        stage = ctx.enter_context(tc.tile_pool(name="stage", bufs=3))
+        result = ctx.enter_context(tc.tile_pool(name="result", bufs=3))
+        psum = ctx.enter_context(tc.psum_pool(name="psum", bufs=8))
+        ctx.enter_context(tc.manual_schedule())
+
+        ident = keep.tile([P, P], F32, name="ident")
+        ones = keep.tile([P, P], BF16, name="ones")
+        brow = keep.tile([P, 3 * FEATURES], BF16, name="brow")
+        bias_sb = keep.tile([P, 3 * FEATURES], BF16, name="bias_sb")
+        x_sb = keep.tile([P, TOK, HIDDEN], BF16, name="x_sb")
+        xg = keep.tile([P, PASSES, TOK, P, 4], BF16, name="xg", align_bytes=64)
+        xc = keep.tile([P, PASSES, TOK * P], U32, name="xc", align_bytes=64)
+        xs = keep.tile([P, PASSES, TOK * P], U8, name="xs", align_bytes=64)
+        wr = [
+            keep.tile([P, PASSES, 4, FEATURES], BF16, name="wr%d" % t) for t in range(3)
+        ]
+        wc = [
+            keep.tile([P, PASSES, N_BLK], U32, name="wc%d" % n, align_bytes=64)
+            for n in range(BLOCKS)
+        ]
+        ws = [
+            keep.tile([P, PASSES, N_BLK], U8, name="ws%d" % n, align_bytes=64)
+            for n in range(BLOCKS)
+        ]
+
+        nc.vector.memset(brow[:].bitcast(I32), 0)
+        nc.vector.memset(ones[:], 1.0)
+        make_identity(nc, ident[:])
+        for t in range(3):
+            nc.scalar.dma_start(
+                out=brow[0:1, t * FEATURES : (t + 1) * FEATURES],
+                in_=biases[t].rearrange("(o n) -> o n", o=1),
+            )
+        for half in range(2):
+            for b in range(BATCH):
+                nc.sync.dma_start(
+                    out=x_sb[b:P:2, 4 * half : 4 * half + 4, :],
+                    in_=hidden_states[b].rearrange("(p j) k -> p j k", j=TOK)[
+                        :, 4 * half : 4 * half + 4, :
+                    ],
+                )
+        for t in range(3):
+            for g in range(PASSES):
+                nc.sync.dma_start(
+                    out=wr[t][:, g].rearrange("p (u e) n -> p u (e n)", u=2),
+                    in_=weights[t][512 * g : 512 * (g + 1), :].rearrange(
+                        "(u p e) n -> p u (e n)", u=2, p=P, e=2
+                    ),
+                )
+
+        x32 = x_sb[:].bitcast(F32)
+        xg32 = xg[:].bitcast(F32)
+
+        def transpose_tokens(j):
+            xt = psum.tile([P, PASSES, 2, P], F32, name="xt", tag="bank")
+            for g in range(PASSES):
+                for u in range(2):
+                    w0 = 256 * g + 128 * u
+                    nc.tensor.transpose(xt[:, g, u, :], x32[:, j, w0 : w0 + P], ident[:])
+            return xt
+
+        def copy_tokens(j, xt):
+            src = xt[:].rearrange("p g u t -> p g t u")
+            if j % 2 == 0:
+                nc.vector.tensor_copy(out=xg32[:, :, j, :, :], in_=src)
+            else:
+                nc.scalar.copy(out=xg32[:, :, j, :, :], in_=src)
+
+        def quantise_tokens(half):
+            for g in range(PASSES):
+                cols = slice(4 * P * half, 4 * P * (half + 1))
+                nc.vector.quantize_mx(
+                    out=xc[:, g, cols].bitcast(FP8X4),
+                    scales=xs[:, g, cols],
+                    in_=xg[:, g, 4 * half : 4 * half + 4].rearrange(
+                        "p j t w -> p (j t w)"
+                    ),
+                )
+
+        for half in range(2):
+            banks = [transpose_tokens(j) for j in range(4 * half, 4 * half + 4)]
+            for i in range(4):
+                copy_tokens(4 * half + i, banks[i])
+            quantise_tokens(half)
+
+        for t in range(3):
+            bp = psum.tile([P, FEATURES], BF16, name="bp", tag="bank")
+            for hf in range(2):
+                nc.tensor.matmul(
+                    out=bp[:, 512 * hf : 512 * (hf + 1)],
+                    lhsT=ones[:],
+                    rhs=brow[:, t * FEATURES + 512 * hf : t * FEATURES + 512 * (hf + 1)],
+                    start=True,
+                    stop=True,
+                )
+            nc.scalar.copy(out=bias_sb[:, t * FEATURES : (t + 1) * FEATURES], in_=bp[:])
+
+        grouped = {}
+
+        def regroup(n, g, engine):
+            if g == 0:
+                grouped[n] = stage.tile(
+                    [P, PASSES, N_BLK, 4], BF16, name="wg", tag="wg", align_bytes=64
+                )
+            t, nb = divmod(n, FEATURES // N_BLK)
+            src = wr[t][:, g, :, nb * N_BLK : (nb + 1) * N_BLK].rearrange(
+                "p t (c i) -> p c t i", i=4
+            )
+            dst = grouped[n][:, g].rearrange("p (c i) t -> p c t i", i=4)
+            if engine == "v":
+                nc.vector.tensor_copy(out=dst, in_=src)
+            else:
+                nc.scalar.copy(out=dst, in_=src)
+
+        def quantise_pass(n, g):
+            nc.vector.quantize_mx(
+                out=wc[n][:, g, :].bitcast(FP8X4),
+                scales=ws[n][:, g, :],
+                in_=grouped[n][:, g].rearrange("p c t -> p (c t)"),
+            )
+
+        def quantise_block(n):
+            nc.vector.quantize_mx(
+                out=wc[n][:].rearrange("p g c -> p (g c)").bitcast(FP8X4),
+                scales=ws[n][:].rearrange("p g c -> p (g c)"),
+                in_=grouped[n][:].rearrange("p g c t -> p (g c t)"),
+            )
+
+        acc = {}
+
+        def mx_pass(n, j, g):
+            if g == 0:
+                acc[(n, j)] = psum.tile([P, N_BLK], F32, name="acc", tag="bank")
+            nc.tensor.matmul_mx(
+                out=acc[(n, j)][:],
+                lhsT=xc[:, g, j * P : (j + 1) * P].bitcast(FP8X4),
+                lhsT_scale=xs[:, g, j * P : (j + 1) * P],
+                rhs=wc[n][:, g, :].bitcast(FP8X4),
+                rhs_scale=ws[n][:, g, :],
+                start=(g == 0),
+                stop=(g == PASSES - 1),
+            )
+
+        res = {}
+
+        def evacuate(n, j, h0, h1):
+            nc.vector.tensor_tensor(
+                out=res[n][:, h0:h1, j, :],
+                in0=acc[(n, j)][:, h0 * HEAD_DIM : h1 * HEAD_DIM].rearrange(
+                    "p (h d) -> p h d", d=HEAD_DIM
+                ),
+                in1=bias_sb[
+                    :, n * N_BLK + h0 * HEAD_DIM : n * N_BLK + h1 * HEAD_DIM
+                ].rearrange("p (h d) -> p h d", d=HEAD_DIM),
+                op=ADD,
+            )
+
+        def store(n, h0, h1):
+            t, nb = divmod(n, FEATURES // N_BLK)
+            for b in range(BATCH):
+                nc.sync.dma_start(
+                    out=outs[t][
+                        b, nb * BLK_HEADS + h0 : nb * BLK_HEADS + h1
+                    ].rearrange("h (p j) d -> p h (j d)", j=TOK),
+                    in_=res[n][b:P:2, h0:h1].rearrange("p h j d -> p h (j d)"),
+                )
+
+        regroup(0, 0, "v")
+        regroup(1, 0, "s")
+        quantise_pass(0, 0)
+        regroup(0, 1, "v")
+        regroup(1, 1, "s")
+        quantise_pass(0, 1)
+        regroup(2, 0, "s")
+        regroup(2, 1, "s")
+        for g in range(PASSES):
+            for j in range(TOK):
+                mx_pass(0, j, g)
+
+        for n in range(BLOCKS):
+            res[n] = result.tile([P, BLK_HEADS, TOK, HEAD_DIM], F32, name="res", tag="res")
+            last = n == BLOCKS - 1
+            if last:
+                for h0 in (0, BLK_HEADS // 2):
+                    for j in range(TOK):
+                        evacuate(n, j, h0, h0 + BLK_HEADS // 2)
+                    store(n, h0, h0 + BLK_HEADS // 2)
+                continue
+            waiting = []
+            for j in range(TOK):
+                if j == Q_POS:
+                    quantise_block(n + 1)
+                    if n + 3 < BLOCKS:
+                        regroup(n + 3, 0, "s")
+                        regroup(n + 3, 1, "s")
+                evacuate(n, j, 0, BLK_HEADS)
+                waiting.append(j)
+                if j >= Q_POS:
+                    for jj in waiting:
+                        for g in range(PASSES):
+                            mx_pass(n + 1, jj, g)
+                    waiting = []
+            store(n, 0, BLK_HEADS)

@@ -20,10 +20,13 @@ HEAD_DIM = 64
 FEATURES = HEADS * HEAD_DIM
 PASSES = HIDDEN // 512
 TOK = 8
+PAIRS = TOK // 2
 N_BLK = 512
-BLK_HEADS = N_BLK // HEAD_DIM
 BLOCKS = 3 * FEATURES // N_BLK
-Q_POS = 4
+N_HALF = 256
+HALF_HEADS = N_HALF // HEAD_DIM
+HALVES = 3 * FEATURES // N_HALF
+Q_AFTER = 4
 
 FLOPS = 2 * BATCH * SEQ * HIDDEN * 3 * FEATURES
 
@@ -39,18 +42,19 @@ def tile_attention_before_kernel(
     with ExitStack() as ctx:
         keep = ctx.enter_context(tc.tile_pool(name="keep", bufs=1))
         stage = ctx.enter_context(tc.tile_pool(name="stage", bufs=3))
-        result = ctx.enter_context(tc.tile_pool(name="result", bufs=3))
+        result = ctx.enter_context(tc.tile_pool(name="result", bufs=6))
         psum = ctx.enter_context(tc.psum_pool(name="psum", bufs=8))
         ctx.enter_context(tc.manual_schedule())
 
         ident = keep.tile([P, P], F32, name="ident")
         ones = keep.tile([P, P], BF16, name="ones")
+        braw = keep.tile([1, 3 * FEATURES], BF16, name="braw")
         brow = keep.tile([P, 3 * FEATURES], BF16, name="brow")
         bias_sb = keep.tile([P, 3 * FEATURES], BF16, name="bias_sb")
         x_sb = keep.tile([P, TOK, HIDDEN], BF16, name="x_sb")
-        xg = keep.tile([P, PASSES, TOK, P, 4], BF16, name="xg", align_bytes=64)
-        xc = keep.tile([P, PASSES, TOK * P], U32, name="xc", align_bytes=64)
-        xs = keep.tile([P, PASSES, TOK * P], U8, name="xs", align_bytes=64)
+        xg = keep.tile([P, PAIRS, PASSES, 2, P, 4], BF16, name="xg", align_bytes=64)
+        xc = keep.tile([P, PAIRS, PASSES, 2 * P], U32, name="xc", align_bytes=64)
+        xs = keep.tile([P, PAIRS, PASSES, 2 * P], U8, name="xs", align_bytes=64)
         wr = [
             keep.tile([P, PASSES, 4, FEATURES], BF16, name="wr%d" % t) for t in range(3)
         ]
@@ -63,23 +67,22 @@ def tile_attention_before_kernel(
             for n in range(BLOCKS)
         ]
 
-        nc.vector.memset(brow[:].bitcast(I32), 0)
-        nc.vector.memset(ones[:], 1.0)
-        make_identity(nc, ident[:])
         for t in range(3):
             nc.scalar.dma_start(
-                out=brow[0:1, t * FEATURES : (t + 1) * FEATURES],
+                out=braw[0:1, t * FEATURES : (t + 1) * FEATURES],
                 in_=biases[t].rearrange("(o n) -> o n", o=1),
             )
-        for half in range(2):
+
+        def load_tokens(q):
             for b in range(BATCH):
                 nc.sync.dma_start(
-                    out=x_sb[b:P:2, 4 * half : 4 * half + 4, :],
+                    out=x_sb[b:P:2, 2 * q : 2 * q + 2, :],
                     in_=hidden_states[b].rearrange("(p j) k -> p j k", j=TOK)[
-                        :, 4 * half : 4 * half + 4, :
+                        :, 2 * q : 2 * q + 2, :
                     ],
                 )
-        for t in range(3):
+
+        def load_weights(t):
             for g in range(PASSES):
                 nc.sync.dma_start(
                     out=wr[t][:, g].rearrange("p (u e) n -> p u (e n)", u=2),
@@ -88,65 +91,74 @@ def tile_attention_before_kernel(
                     ),
                 )
 
+        load_tokens(0)
+        load_weights(0)
+        for q in range(1, PAIRS):
+            load_tokens(q)
+        load_weights(1)
+        load_weights(2)
+
+        nc.vector.memset(brow[:].bitcast(I32), 0)
+        nc.vector.memset(ones[:], 1.0)
+        make_identity(nc, ident[:])
+        nc.vector.tensor_copy(out=brow[0:1, :], in_=braw[0:1, :])
+
         x32 = x_sb[:].bitcast(F32)
         xg32 = xg[:].bitcast(F32)
+        banks = {}
 
         def transpose_tokens(j):
-            xt = psum.tile([P, PASSES, 2, P], F32, name="xt", tag="bank")
+            banks[j] = psum.tile([P, PASSES, 2, P], F32, name="xt", tag="bank")
             for g in range(PASSES):
                 for u in range(2):
                     w0 = 256 * g + 128 * u
-                    nc.tensor.transpose(xt[:, g, u, :], x32[:, j, w0 : w0 + P], ident[:])
-            return xt
+                    nc.tensor.transpose(
+                        banks[j][:, g, u, :], x32[:, j, w0 : w0 + P], ident[:]
+                    )
 
-        def copy_tokens(j, xt):
-            src = xt[:].rearrange("p g u t -> p g t u")
-            if j % 2 == 0:
-                nc.vector.tensor_copy(out=xg32[:, :, j, :, :], in_=src)
+        def copy_tokens(j, engine):
+            src = banks[j][:].rearrange("p g u t -> p g t u")
+            dst = xg32[:, j // 2, :, j % 2, :, :]
+            if engine == "v":
+                nc.vector.tensor_copy(out=dst, in_=src)
             else:
-                nc.scalar.copy(out=xg32[:, :, j, :, :], in_=src)
+                nc.scalar.copy(out=dst, in_=src)
 
-        def quantise_tokens(half):
-            for g in range(PASSES):
-                cols = slice(4 * P * half, 4 * P * (half + 1))
-                nc.vector.quantize_mx(
-                    out=xc[:, g, cols].bitcast(FP8X4),
-                    scales=xs[:, g, cols],
-                    in_=xg[:, g, 4 * half : 4 * half + 4].rearrange(
-                        "p j t w -> p (j t w)"
-                    ),
+        def quantise_tokens(q):
+            nc.vector.quantize_mx(
+                out=xc[:, q].rearrange("p g c -> p (g c)").bitcast(FP8X4),
+                scales=xs[:, q].rearrange("p g c -> p (g c)"),
+                in_=xg[:, q].rearrange("p g j t w -> p (g j t w)"),
+            )
+
+        def spread_biases():
+            for t in range(3):
+                bp = psum.tile([P, FEATURES], BF16, name="bp", tag="bank")
+                for hf in range(2):
+                    c0 = t * FEATURES + 512 * hf
+                    nc.tensor.matmul(
+                        out=bp[:, 512 * hf : 512 * (hf + 1)],
+                        lhsT=ones[:],
+                        rhs=brow[:, c0 : c0 + 512],
+                        start=True,
+                        stop=True,
+                    )
+                nc.scalar.copy(
+                    out=bias_sb[:, t * FEATURES : (t + 1) * FEATURES], in_=bp[:]
                 )
-
-        for half in range(2):
-            banks = [transpose_tokens(j) for j in range(4 * half, 4 * half + 4)]
-            for i in range(4):
-                copy_tokens(4 * half + i, banks[i])
-            quantise_tokens(half)
-
-        for t in range(3):
-            bp = psum.tile([P, FEATURES], BF16, name="bp", tag="bank")
-            for hf in range(2):
-                nc.tensor.matmul(
-                    out=bp[:, 512 * hf : 512 * (hf + 1)],
-                    lhsT=ones[:],
-                    rhs=brow[:, t * FEATURES + 512 * hf : t * FEATURES + 512 * (hf + 1)],
-                    start=True,
-                    stop=True,
-                )
-            nc.scalar.copy(out=bias_sb[:, t * FEATURES : (t + 1) * FEATURES], in_=bp[:])
 
         grouped = {}
 
-        def regroup(n, g, engine):
-            if g == 0:
+        def regroup(n, g, engine, c0=0, c1=N_BLK):
+            if n not in grouped:
                 grouped[n] = stage.tile(
                     [P, PASSES, N_BLK, 4], BF16, name="wg", tag="wg", align_bytes=64
                 )
             t, nb = divmod(n, FEATURES // N_BLK)
-            src = wr[t][:, g, :, nb * N_BLK : (nb + 1) * N_BLK].rearrange(
+            src = wr[t][:, g, :, nb * N_BLK + c0 : nb * N_BLK + c1].rearrange(
                 "p t (c i) -> p c t i", i=4
             )
-            dst = grouped[n][:, g].rearrange("p (c i) t -> p c t i", i=4)
+            dst = grouped[n][:, g, c0:c1, :].rearrange("p (c i) t -> p c t i", i=4)
             if engine == "v":
                 nc.vector.tensor_copy(out=dst, in_=src)
             else:
@@ -168,76 +180,105 @@ def tile_attention_before_kernel(
 
         acc = {}
 
-        def mx_pass(n, j, g):
-            if g == 0:
-                acc[(n, j)] = psum.tile([P, N_BLK], F32, name="acc", tag="bank")
-            nc.tensor.matmul_mx(
-                out=acc[(n, j)][:],
-                lhsT=xc[:, g, j * P : (j + 1) * P].bitcast(FP8X4),
-                lhsT_scale=xs[:, g, j * P : (j + 1) * P],
-                rhs=wc[n][:, g, :].bitcast(FP8X4),
-                rhs_scale=ws[n][:, g, :],
-                start=(g == 0),
-                stop=(g == PASSES - 1),
-            )
+        def multiply(h, q):
+            acc[(h, q)] = psum.tile([P, 2, N_HALF], F32, name="acc", tag="bank")
+            n, hf = divmod(h, 2)
+            cols = slice(hf * N_HALF, (hf + 1) * N_HALF)
+            for jj in range(2):
+                toks = slice(jj * P, (jj + 1) * P)
+                for g in range(PASSES):
+                    nc.tensor.matmul_mx(
+                        out=acc[(h, q)][:, jj, :],
+                        lhsT=xc[:, q, g, toks].bitcast(FP8X4),
+                        lhsT_scale=xs[:, q, g, toks],
+                        rhs=wc[n][:, g, cols].bitcast(FP8X4),
+                        rhs_scale=ws[n][:, g, cols],
+                        start=(g == 0),
+                        stop=(g == PASSES - 1),
+                    )
 
         res = {}
 
-        def evacuate(n, j, h0, h1):
+        def evacuate(h, q):
+            if h not in res:
+                res[h] = result.tile(
+                    [P, HALF_HEADS, TOK, HEAD_DIM], F32, name="res", tag="res"
+                )
             nc.vector.tensor_tensor(
-                out=res[n][:, h0:h1, j, :],
-                in0=acc[(n, j)][:, h0 * HEAD_DIM : h1 * HEAD_DIM].rearrange(
-                    "p (h d) -> p h d", d=HEAD_DIM
-                ),
-                in1=bias_sb[
-                    :, n * N_BLK + h0 * HEAD_DIM : n * N_BLK + h1 * HEAD_DIM
-                ].rearrange("p (h d) -> p h d", d=HEAD_DIM),
+                out=res[h][:, :, 2 * q : 2 * q + 2, :].rearrange("p h j d -> p j h d"),
+                in0=acc[(h, q)][:].rearrange("p j (h d) -> p j h d", d=HEAD_DIM),
+                in1=bias_sb[:, h * N_HALF : (h + 1) * N_HALF]
+                .rearrange("p (h d) -> p h d", d=HEAD_DIM)
+                .unsqueeze(1)
+                .to_broadcast([P, 2, HALF_HEADS, HEAD_DIM]),
                 op=ADD,
             )
 
-        def store(n, h0, h1):
-            t, nb = divmod(n, FEATURES // N_BLK)
+        def store(h):
+            t, hh = divmod(h, FEATURES // N_HALF)
             for b in range(BATCH):
                 nc.sync.dma_start(
                     out=outs[t][
-                        b, nb * BLK_HEADS + h0 : nb * BLK_HEADS + h1
+                        b, hh * HALF_HEADS : (hh + 1) * HALF_HEADS
                     ].rearrange("h (p j) d -> p h (j d)", j=TOK),
-                    in_=res[n][b:P:2, h0:h1].rearrange("p h j d -> p h (j d)"),
+                    in_=res[h][b:P:2].rearrange("p h j d -> p h (j d)"),
                 )
 
+        transpose_tokens(0)
+        transpose_tokens(1)
+        copy_tokens(0, "v")
+        copy_tokens(1, "s")
+        quantise_tokens(0)
+        spread_biases()
         regroup(0, 0, "v")
         regroup(1, 0, "s")
         quantise_pass(0, 0)
         regroup(0, 1, "v")
-        regroup(1, 1, "s")
         quantise_pass(0, 1)
-        regroup(2, 0, "s")
-        regroup(2, 1, "s")
-        for g in range(PASSES):
-            for j in range(TOK):
-                mx_pass(0, j, g)
+        for q in range(1, PAIRS):
+            transpose_tokens(2 * q)
+            transpose_tokens(2 * q + 1)
+            if q >= 2:
+                evacuate(0, q - 2)
+                evacuate(1, q - 2)
+            copy_tokens(2 * q, "v")
+            copy_tokens(2 * q + 1, "s")
+            quantise_tokens(q)
+            multiply(0, q - 1)
+            multiply(1, q - 1)
+            if q < PAIRS - 1:
+                regroup(1, 1, "s", (q - 1) * N_HALF, q * N_HALF)
+        multiply(0, PAIRS - 1)
+        multiply(1, PAIRS - 1)
+        evacuate(0, 2)
+        evacuate(1, 2)
+        quantise_block(1)
+        for q in range(3):
+            multiply(2, q)
+        evacuate(0, 3)
+        store(0)
+        multiply(2, 3)
+        evacuate(1, 3)
+        store(1)
+        for q in range(PAIRS):
+            multiply(3, q)
+        for n in (2, 3):
+            for g in range(PASSES):
+                regroup(n, g, "s")
 
-        for n in range(BLOCKS):
-            res[n] = result.tile([P, BLK_HEADS, TOK, HEAD_DIM], F32, name="res", tag="res")
-            last = n == BLOCKS - 1
-            if last:
-                for h0 in (0, BLK_HEADS // 2):
-                    for j in range(TOK):
-                        evacuate(n, j, h0, h0 + BLK_HEADS // 2)
-                    store(n, h0, h0 + BLK_HEADS // 2)
-                continue
-            waiting = []
-            for j in range(TOK):
-                if j == Q_POS:
+        for n in range(1, BLOCKS):
+            more = n + 1 < BLOCKS
+            for k in range(2 * PAIRS):
+                h, q = 2 * n + k // PAIRS, k % PAIRS
+                if more and k == Q_AFTER:
                     quantise_block(n + 1)
                     if n + 3 < BLOCKS:
-                        regroup(n + 3, 0, "s")
-                        regroup(n + 3, 1, "s")
-                evacuate(n, j, 0, BLK_HEADS)
-                waiting.append(j)
-                if j >= Q_POS:
-                    for jj in waiting:
                         for g in range(PASSES):
-                            mx_pass(n + 1, jj, g)
-                    waiting = []
-            store(n, 0, BLK_HEADS)
+                            regroup(n + 3, g, "s")
+                    for kk in range(k):
+                        multiply(2 * n + 2 + kk // PAIRS, kk % PAIRS)
+                evacuate(h, q)
+                if more and k >= Q_AFTER:
+                    multiply(h + 2, q)
+                if q == PAIRS - 1:
+                    store(h)

@@ -51,12 +51,22 @@ def tile_attention_before_kernel(
         braw = keep.tile([1, 3 * FEATURES], BF16, name="braw")
         brow = keep.tile([P, 3 * FEATURES], BF16, name="brow")
         bias_sb = keep.tile([P, 3 * FEATURES], BF16, name="bias_sb")
-        x_sb = keep.tile([P, TOK, HIDDEN], BF16, name="x_sb")
-        xg = keep.tile([P, PAIRS, PASSES, 2, P, 4], BF16, name="xg", align_bytes=64)
-        xc = keep.tile([P, PAIRS, PASSES, 2 * P], U32, name="xc", align_bytes=64)
-        xs = keep.tile([P, PAIRS, PASSES, 2 * P], U8, name="xs", align_bytes=64)
+        x_sb = [keep.tile([P, 2, HIDDEN], BF16, name="x_sb%d" % q) for q in range(PAIRS)]
+        xg = [
+            keep.tile([P, 2, PASSES, P, 4], BF16, name="xg%d" % q, align_bytes=64)
+            for q in range(PAIRS)
+        ]
+        xc = [
+            keep.tile([P, 2, PASSES, P], U32, name="xc%d" % q, align_bytes=64)
+            for q in range(PAIRS)
+        ]
+        xs = [
+            keep.tile([P, 2, PASSES, P], U8, name="xs%d" % q, align_bytes=64)
+            for q in range(PAIRS)
+        ]
         wr = [
-            keep.tile([P, PASSES, 4, FEATURES], BF16, name="wr%d" % t) for t in range(3)
+            [keep.tile([P, 4, FEATURES], BF16, name="wr%d%d" % (t, g)) for g in range(PASSES)]
+            for t in range(3)
         ]
         wc = [
             keep.tile([P, PASSES, N_BLK], U32, name="wc%d" % n, align_bytes=64)
@@ -76,7 +86,7 @@ def tile_attention_before_kernel(
         def load_tokens(q):
             for b in range(BATCH):
                 nc.sync.dma_start(
-                    out=x_sb[b:P:2, 2 * q : 2 * q + 2, :],
+                    out=x_sb[q][b:P:2, :, :],
                     in_=hidden_states[b].rearrange("(p j) k -> p j k", j=TOK)[
                         :, 2 * q : 2 * q + 2, :
                     ],
@@ -85,7 +95,7 @@ def tile_attention_before_kernel(
         def load_weights(t):
             for g in range(PASSES):
                 nc.sync.dma_start(
-                    out=wr[t][:, g].rearrange("p (u e) n -> p u (e n)", u=2),
+                    out=wr[t][g][:].rearrange("p (u e) n -> p u (e n)", u=2),
                     in_=weights[t][512 * g : 512 * (g + 1), :].rearrange(
                         "(u p e) n -> p u (e n)", u=2, p=P, e=2
                     ),
@@ -103,8 +113,6 @@ def tile_attention_before_kernel(
         make_identity(nc, ident[:])
         nc.vector.tensor_copy(out=brow[0:1, :], in_=braw[0:1, :])
 
-        x32 = x_sb[:].bitcast(F32)
-        xg32 = xg[:].bitcast(F32)
         banks = {}
 
         def transpose_tokens(j):
@@ -113,12 +121,14 @@ def tile_attention_before_kernel(
                 for u in range(2):
                     w0 = 256 * g + 128 * u
                     nc.tensor.transpose(
-                        banks[j][:, g, u, :], x32[:, j, w0 : w0 + P], ident[:]
+                        banks[j][:, g, u, :],
+                        x_sb[j // 2][:].bitcast(F32)[:, j % 2, w0 : w0 + P],
+                        ident[:],
                     )
 
         def copy_tokens(j, engine):
             src = banks[j][:].rearrange("p g u t -> p g t u")
-            dst = xg32[:, j // 2, :, j % 2, :, :]
+            dst = xg[j // 2][:].bitcast(F32)[:, j % 2]
             if engine == "v":
                 nc.vector.tensor_copy(out=dst, in_=src)
             else:
@@ -126,9 +136,9 @@ def tile_attention_before_kernel(
 
         def quantise_tokens(q):
             nc.vector.quantize_mx(
-                out=xc[:, q].rearrange("p g c -> p (g c)").bitcast(FP8X4),
-                scales=xs[:, q].rearrange("p g c -> p (g c)"),
-                in_=xg[:, q].rearrange("p g j t w -> p (g j t w)"),
+                out=xc[q][:].rearrange("p j g c -> p (j g c)").bitcast(FP8X4),
+                scales=xs[q][:].rearrange("p j g c -> p (j g c)"),
+                in_=xg[q][:].rearrange("p j g t w -> p (j g t w)"),
             )
 
         def spread_biases():
@@ -155,7 +165,7 @@ def tile_attention_before_kernel(
                     [P, PASSES, N_BLK, 4], BF16, name="wg", tag="wg", align_bytes=64
                 )
             t, nb = divmod(n, FEATURES // N_BLK)
-            src = wr[t][:, g, :, nb * N_BLK + c0 : nb * N_BLK + c1].rearrange(
+            src = wr[t][g][:, :, nb * N_BLK + c0 : nb * N_BLK + c1].rearrange(
                 "p t (c i) -> p c t i", i=4
             )
             dst = grouped[n][:, g, c0:c1, :].rearrange("p (c i) t -> p c t i", i=4)
@@ -185,12 +195,11 @@ def tile_attention_before_kernel(
             n, hf = divmod(h, 2)
             cols = slice(hf * N_HALF, (hf + 1) * N_HALF)
             for jj in range(2):
-                toks = slice(jj * P, (jj + 1) * P)
                 for g in range(PASSES):
                     nc.tensor.matmul_mx(
                         out=acc[(h, q)][:, jj, :],
-                        lhsT=xc[:, q, g, toks].bitcast(FP8X4),
-                        lhsT_scale=xs[:, q, g, toks],
+                        lhsT=xc[q][:, jj, g, :].bitcast(FP8X4),
+                        lhsT_scale=xs[q][:, jj, g, :],
                         rhs=wc[n][:, g, cols].bitcast(FP8X4),
                         rhs_scale=ws[n][:, g, cols],
                         start=(g == 0),

@@ -213,15 +213,19 @@ def tile_attention_before_kernel(
                 res[h] = result.tile(
                     [P, HALF_HEADS, TOK, HEAD_DIM], F32, name="res", tag="res"
                 )
-            nc.vector.tensor_tensor(
-                out=res[h][:, :, 2 * q : 2 * q + 2, :].rearrange("p h j d -> p j h d"),
-                in0=acc[(h, q)][:].rearrange("p j (h d) -> p j h d", d=HEAD_DIM),
-                in1=bias_sb[:, h * N_HALF : (h + 1) * N_HALF]
+            dst = res[h][:, :, 2 * q : 2 * q + 2, :].rearrange("p h j d -> p j h d")
+            sums = acc[(h, q)][:].rearrange("p j (h d) -> p j h d", d=HEAD_DIM)
+            bias = (
+                bias_sb[:, h * N_HALF : (h + 1) * N_HALF]
                 .rearrange("p (h d) -> p h d", d=HEAD_DIM)
                 .unsqueeze(1)
-                .to_broadcast([P, 2, HALF_HEADS, HEAD_DIM]),
-                op=ADD,
+                .to_broadcast([P, 2, HALF_HEADS, HEAD_DIM])
             )
+            if q == 0 and (h >= 8 or (h >= 4 and h % 2 == 0)):
+                nc.scalar.copy(out=dst, in_=sums)
+                nc.gpsimd.tensor_tensor(out=dst, in0=dst, in1=bias, op=ADD)
+            else:
+                nc.vector.tensor_tensor(out=dst, in0=sums, in1=bias, op=ADD)
 
         def store(h):
             t, hh = divmod(h, FEATURES // N_HALF)
@@ -271,19 +275,17 @@ def tile_attention_before_kernel(
         store(1)
         for q in range(PAIRS):
             multiply(3, q)
-        for n in (2, 3):
-            for g in range(PASSES):
-                regroup(n, g, "s")
+        for g in range(PASSES):
+            regroup(2, g, "s")
 
         for n in range(1, BLOCKS):
             more = n + 1 < BLOCKS
             for k in range(2 * PAIRS):
                 h, q = 2 * n + k // PAIRS, k % PAIRS
+                if n + 2 < BLOCKS and q == 0:
+                    regroup(n + 2, k // PAIRS, "s")
                 if more and k == Q_AFTER:
                     quantise_block(n + 1)
-                    if n + 3 < BLOCKS:
-                        for g in range(PASSES):
-                            regroup(n + 3, g, "s")
                     for kk in range(k):
                         multiply(2 * n + 2 + kk // PAIRS, kk % PAIRS)
                 evacuate(h, q)

@@ -101,12 +101,10 @@ def tile_attention_before_kernel(
                     ),
                 )
 
-        load_tokens(0)
-        load_weights(0)
-        for q in range(1, PAIRS):
+        for q in range(PAIRS):
             load_tokens(q)
-        load_weights(1)
-        load_weights(2)
+        for t in range(3):
+            load_weights(t)
 
         nc.vector.memset(brow[:].bitcast(I32), 0)
         nc.vector.memset(ones[:], 1.0)
@@ -237,41 +235,32 @@ def tile_attention_before_kernel(
                     in_=res[h][b:P:2].rearrange("p h j d -> p h (j d)"),
                 )
 
-        transpose_tokens(0)
-        transpose_tokens(1)
-        copy_tokens(0, "v")
-        copy_tokens(1, "s")
-        quantise_tokens(0)
+        for q in range(PAIRS):
+            transpose_tokens(2 * q)
+            transpose_tokens(2 * q + 1)
+            copy_tokens(2 * q, "v")
+            copy_tokens(2 * q + 1, "s")
+            if q >= 1:
+                quantise_tokens(q - 1)
         spread_biases()
+        quantise_tokens(PAIRS - 1)
         regroup(0, 0, "v")
         regroup(1, 0, "s")
         quantise_pass(0, 0)
         regroup(0, 1, "v")
+        regroup(1, 1, "s")
         quantise_pass(0, 1)
-        for q in range(1, PAIRS):
-            transpose_tokens(2 * q)
-            transpose_tokens(2 * q + 1)
-            if q >= 2:
-                evacuate(0, q - 2)
-                evacuate(1, q - 2)
-            copy_tokens(2 * q, "v")
-            copy_tokens(2 * q + 1, "s")
-            quantise_tokens(q)
-            multiply(0, q - 1)
-            multiply(1, q - 1)
-            if q < PAIRS - 1:
-                regroup(1, 1, "s", (q - 1) * N_HALF, q * N_HALF)
-        multiply(0, PAIRS - 1)
-        multiply(1, PAIRS - 1)
-        evacuate(0, 2)
-        evacuate(1, 2)
-        quantise_block(1)
-        for q in range(3):
-            multiply(2, q)
-        evacuate(0, 3)
+        for h in range(2):
+            for q in range(PAIRS):
+                multiply(h, q)
+        for q in range(PAIRS):
+            evacuate(0, q)
         store(0)
-        multiply(2, 3)
-        evacuate(1, 3)
+        quantise_block(1)
+        for q in range(PAIRS):
+            multiply(2, q)
+        for q in range(PAIRS):
+            evacuate(1, q)
         store(1)
         for q in range(PAIRS):
             multiply(3, q)

@@ -95,9 +95,9 @@ def tile_attention_before_kernel(
         def load_weights(t):
             for g in range(PASSES):
                 nc.sync.dma_start(
-                    out=wr[t][g][:].rearrange("p (u e) n -> p u (e n)", u=2),
+                    out=wr[t][g][:],
                     in_=weights[t][512 * g : 512 * (g + 1), :].rearrange(
-                        "(u p e) n -> p u (e n)", u=2, p=P, e=2
+                        "(p t) n -> p t n", t=4
                     ),
                 )
 
@@ -117,10 +117,11 @@ def tile_attention_before_kernel(
             banks[j] = psum.tile([P, PASSES, 2, P], F32, name="xt", tag="bank")
             for g in range(PASSES):
                 for u in range(2):
-                    w0 = 256 * g + 128 * u
                     nc.tensor.transpose(
                         banks[j][:, g, u, :],
-                        x_sb[j // 2][:].bitcast(F32)[:, j % 2, w0 : w0 + P],
+                        x_sb[j // 2][:].bitcast(F32)[
+                            :, j % 2, 256 * g + u : 256 * (g + 1) : 2
+                        ],
                         ident[:],
                     )
 
@@ -219,7 +220,7 @@ def tile_attention_before_kernel(
                 .unsqueeze(1)
                 .to_broadcast([P, 2, HALF_HEADS, HEAD_DIM])
             )
-            if q == 0 and (h >= 8 or (h >= 4 and h % 2 == 0)):
+            if (q == 0 and (h >= 8 or (h >= 2 and h % 2 == 0))) or (h, q) == (8, 2):
                 nc.scalar.copy(out=dst, in_=sums)
                 nc.gpsimd.tensor_tensor(out=dst, in0=dst, in1=bias, op=ADD)
             else:

from contextlib import ExitStack

import concourse.mybir as mybir
from concourse.masks import make_identity

F32 = mybir.dt.float32
BF16 = mybir.dt.bfloat16
U32 = mybir.dt.uint32
U8 = mybir.dt.uint8
I32 = mybir.dt.int32
FP8X4 = mybir.dt.float8_e4m3fn_x4
ADD = mybir.AluOpType.add

P = 128
BATCH = 2
SEQ = 512
HIDDEN = 1024
HEADS = 16
HEAD_DIM = 64
FEATURES = HEADS * HEAD_DIM
PASSES = HIDDEN // 512
TOK = 8
PAIRS = TOK // 2
N_BLK = 512
BLOCKS = 3 * FEATURES // N_BLK
N_HALF = 256
HALF_HEADS = N_HALF // HEAD_DIM
HALVES = 3 * FEATURES // N_HALF
Q_AFTER = 4

FLOPS = 2 * BATCH * SEQ * HIDDEN * 3 * FEATURES


def tile_attention_before_kernel(
    tc, hidden_states, Wq, bq, Wk, bk, Wv, bv, out_0, out_1, out_2
):
    nc = tc.nc
    weights = (Wq, Wk, Wv)
    biases = (bq, bk, bv)
    outs = (out_0, out_1, out_2)

    with ExitStack() as ctx:
        keep = ctx.enter_context(tc.tile_pool(name="keep", bufs=1))
        stage = ctx.enter_context(tc.tile_pool(name="stage", bufs=3))
        result = ctx.enter_context(tc.tile_pool(name="result", bufs=6))
        psum = ctx.enter_context(tc.psum_pool(name="psum", bufs=8))
        ctx.enter_context(tc.manual_schedule())

        ident = keep.tile([P, P], F32, name="ident")
        ones = keep.tile([P, P], BF16, name="ones")
        braw = keep.tile([1, 3 * FEATURES], BF16, name="braw")
        brow = keep.tile([P, 3 * FEATURES], BF16, name="brow")
        bias_sb = keep.tile([P, 3 * FEATURES], BF16, name="bias_sb")
        x_sb = [keep.tile([P, 2, HIDDEN], BF16, name="x_sb%d" % q) for q in range(PAIRS)]
        xg = [
            keep.tile([P, 2, PASSES, P, 4], BF16, name="xg%d" % q, align_bytes=64)
            for q in range(PAIRS)
        ]
        xc = [
            keep.tile([P, 2, PASSES, P], U32, name="xc%d" % q, align_bytes=64)
            for q in range(PAIRS)
        ]
        xs = [
            keep.tile([P, 2, PASSES, P], U8, name="xs%d" % q, align_bytes=64)
            for q in range(PAIRS)
        ]
        wr = [
            [keep.tile([P, 4, FEATURES], BF16, name="wr%d%d" % (t, g)) for g in range(PASSES)]
            for t in range(3)
        ]
        wc = [
            keep.tile([P, PASSES, N_BLK], U32, name="wc%d" % n, align_bytes=64)
            for n in range(BLOCKS)
        ]
        ws = [
            keep.tile([P, PASSES, N_BLK], U8, name="ws%d" % n, align_bytes=64)
            for n in range(BLOCKS)
        ]

        for t in range(3):
            nc.scalar.dma_start(
                out=braw[0:1, t * FEATURES : (t + 1) * FEATURES],
                in_=biases[t].rearrange("(o n) -> o n", o=1),
            )

        def load_tokens(q):
            for b in range(BATCH):
                nc.sync.dma_start(
                    out=x_sb[q][b:P:2, :, :],
                    in_=hidden_states[b].rearrange("(p j) k -> p j k", j=TOK)[
                        :, 2 * q : 2 * q + 2, :
                    ],
                )

        def load_weights(t):
            for g in range(PASSES):
                nc.sync.dma_start(
                    out=wr[t][g][:],
                    in_=weights[t][512 * g : 512 * (g + 1), :].rearrange(
                        "(p t) n -> p t n", t=4
                    ),
                )

        for q in range(PAIRS):
            load_tokens(q)
        for t in range(3):
            load_weights(t)

        nc.vector.memset(brow[:].bitcast(I32), 0)
        nc.vector.memset(ones[:], 1.0)
        make_identity(nc, ident[:])
        nc.vector.tensor_copy(out=brow[0:1, :], in_=braw[0:1, :])

        banks = {}

        def transpose_tokens(j):
            banks[j] = psum.tile([P, PASSES, 2, P], F32, name="xt", tag="bank")
            for g in range(PASSES):
                for u in range(2):
                    nc.tensor.transpose(
                        banks[j][:, g, u, :],
                        x_sb[j // 2][:].bitcast(F32)[
                            :, j % 2, 256 * g + u : 256 * (g + 1) : 2
                        ],
                        ident[:],
                    )

        def copy_tokens(j, engine):
            src = banks[j][:].rearrange("p g u t -> p g t u")
            dst = xg[j // 2][:].bitcast(F32)[:, j % 2]
            if engine == "v":
                nc.vector.tensor_copy(out=dst, in_=src)
            else:
                nc.scalar.copy(out=dst, in_=src)

        def quantise_tokens(q):
            nc.vector.quantize_mx(
                out=xc[q][:].rearrange("p j g c -> p (j g c)").bitcast(FP8X4),
                scales=xs[q][:].rearrange("p j g c -> p (j g c)"),
                in_=xg[q][:].rearrange("p j g t w -> p (j g t w)"),
            )

        def spread_biases():
            for t in range(3):
                bp = psum.tile([P, FEATURES], BF16, name="bp", tag="bank")
                for hf in range(2):
                    c0 = t * FEATURES + 512 * hf
                    nc.tensor.matmul(
                        out=bp[:, 512 * hf : 512 * (hf + 1)],
                        lhsT=ones[:],
                        rhs=brow[:, c0 : c0 + 512],
                        start=True,
                        stop=True,
                    )
                nc.scalar.copy(
                    out=bias_sb[:, t * FEATURES : (t + 1) * FEATURES], in_=bp[:]
                )

        grouped = {}

        def regroup(n, g, engine, c0=0, c1=N_BLK):
            if n not in grouped:
                grouped[n] = stage.tile(
                    [P, PASSES, N_BLK, 4], BF16, name="wg", tag="wg", align_bytes=64
                )
            t, nb = divmod(n, FEATURES // N_BLK)
            src = wr[t][g][:, :, nb * N_BLK + c0 : nb * N_BLK + c1].rearrange(
                "p t (c i) -> p c t i", i=4
            )
            dst = grouped[n][:, g, c0:c1, :].rearrange("p (c i) t -> p c t i", i=4)
            if engine == "v":
                nc.vector.tensor_copy(out=dst, in_=src)
            else:
                nc.scalar.copy(out=dst, in_=src)

        def quantise_pass(n, g):
            nc.vector.quantize_mx(
                out=wc[n][:, g, :].bitcast(FP8X4),
                scales=ws[n][:, g, :],
                in_=grouped[n][:, g].rearrange("p c t -> p (c t)"),
            )

        def quantise_block(n):
            nc.vector.quantize_mx(
                out=wc[n][:].rearrange("p g c -> p (g c)").bitcast(FP8X4),
                scales=ws[n][:].rearrange("p g c -> p (g c)"),
                in_=grouped[n][:].rearrange("p g c t -> p (g c t)"),
            )

        acc = {}

        def multiply(h, q):
            acc[(h, q)] = psum.tile([P, 2, N_HALF], F32, name="acc", tag="bank")
            n, hf = divmod(h, 2)
            cols = slice(hf * N_HALF, (hf + 1) * N_HALF)
            for jj in range(2):
                for g in range(PASSES):
                    nc.tensor.matmul_mx(
                        out=acc[(h, q)][:, jj, :],
                        lhsT=xc[q][:, jj, g, :].bitcast(FP8X4),
                        lhsT_scale=xs[q][:, jj, g, :],
                        rhs=wc[n][:, g, cols].bitcast(FP8X4),
                        rhs_scale=ws[n][:, g, cols],
                        start=(g == 0),
                        stop=(g == PASSES - 1),
                    )

        res = {}

        def evacuate(h, q):
            if h not in res:
                res[h] = result.tile(
                    [P, HALF_HEADS, TOK, HEAD_DIM], F32, name="res", tag="res"
                )
            dst = res[h][:, :, 2 * q : 2 * q + 2, :].rearrange("p h j d -> p j h d")
            sums = acc[(h, q)][:].rearrange("p j (h d) -> p j h d", d=HEAD_DIM)
            bias = (
                bias_sb[:, h * N_HALF : (h + 1) * N_HALF]
                .rearrange("p (h d) -> p h d", d=HEAD_DIM)
                .unsqueeze(1)
                .to_broadcast([P, 2, HALF_HEADS, HEAD_DIM])
            )
            if (q == 0 and (h >= 8 or (h >= 2 and h % 2 == 0))) or (h, q) == (8, 2):
                nc.scalar.copy(out=dst, in_=sums)
                nc.gpsimd.tensor_tensor(out=dst, in0=dst, in1=bias, op=ADD)
            else:
                nc.vector.tensor_tensor(out=dst, in0=sums, in1=bias, op=ADD)

        def store(h):
            t, hh = divmod(h, FEATURES // N_HALF)
            for b in range(BATCH):
                nc.sync.dma_start(
                    out=outs[t][
                        b, hh * HALF_HEADS : (hh + 1) * HALF_HEADS
                    ].rearrange("h (p j) d -> p h (j d)", j=TOK),
                    in_=res[h][b:P:2].rearrange("p h j d -> p h (j d)"),
                )

        for q in range(PAIRS):
            transpose_tokens(2 * q)
            transpose_tokens(2 * q + 1)
            copy_tokens(2 * q, "v")
            copy_tokens(2 * q + 1, "s")
            if q >= 1:
                quantise_tokens(q - 1)
        spread_biases()
        quantise_tokens(PAIRS - 1)
        regroup(0, 0, "v")
        regroup(1, 0, "s")
        quantise_pass(0, 0)
        regroup(0, 1, "v")
        regroup(1, 1, "s")
        quantise_pass(0, 1)
        for h in range(2):
            for q in range(PAIRS):
                multiply(h, q)
        for q in range(PAIRS):
            evacuate(0, q)
        store(0)
        quantise_block(1)
        for q in range(PAIRS):
            multiply(2, q)
        for q in range(PAIRS):
            evacuate(1, q)
        store(1)
        for q in range(PAIRS):
            multiply(3, q)
        for g in range(PASSES):
            regroup(2, g, "s")

        for n in range(1, BLOCKS):
            more = n + 1 < BLOCKS
            for k in range(2 * PAIRS):
                h, q = 2 * n + k // PAIRS, k % PAIRS
                if n + 2 < BLOCKS and q == 0:
                    regroup(n + 2, k // PAIRS, "s")
                if more and k == Q_AFTER:
                    quantise_block(n + 1)
                    for kk in range(k):
                        multiply(2 * n + 2 + kk // PAIRS, kk % PAIRS)
                evacuate(h, q)
                if more and k >= Q_AFTER:
                    multiply(h + 2, q)
                if q == PAIRS - 1:
                    store(h)
